import numpy as np
import ml_dtypes


def mxq(x, axis, fmt="e4m3"):
    dtype, down = {"e4m3": (ml_dtypes.float8_e4m3fn, 7), "e5m2": (ml_dtypes.float8_e5m2, 14)}[fmt]
    v = np.moveaxis(np.asarray(x, np.float32).astype(ml_dtypes.bfloat16).astype(np.float64), axis, -1)
    blocks = v.reshape(v.shape[:-1] + (-1, 32))
    amax = np.abs(blocks).max(-1, keepdims=True)
    byte = np.maximum(np.where(amax > 0, np.frexp(amax)[1] - 1 + 127, 0) - down, 1)
    scale = np.exp2(byte - 127.0)
    codes = (blocks / scale).astype(np.float32).astype(dtype).astype(np.float64)
    return np.moveaxis((codes * scale).reshape(v.shape), -1, axis)


WIDE = False


def mx_kscale(k):
    if not WIDE:
        return np.ones(k)
    levels = np.array([10, -10, 5, -5, 0])
    a = np.random.permutation(np.resize(levels, k // 512 * 4)).reshape(k // 512, 4)
    idx = np.arange(k)
    return np.exp2(a[idx // 512, idx % 128 // 32])


BF16 = ml_dtypes.bfloat16


def bf(x):
    return np.asarray(x, np.float32).astype(BF16)


def f64(x):
    return np.asarray(x).astype(np.float64)


B, H, W, CH, NC, DIM = 4, 16, 16, 512, 22, 512


def _patches3x3(a):
    b, h, w, c = a.shape
    p = np.pad(a, ((0, 0), (1, 1), (1, 1), (0, 0)))
    return np.stack([p[:, i:i + h, j:j + w, :] for i in range(3) for j in range(3)], axis=3)


def setup_inputs():
    s = mx_kscale(CH)
    lim = np.sqrt(6.0 / (CH * 9))
    return {"x": bf(np.random.standard_normal((B, H, W, CH)) * s),
            "seg_mask": bf(np.random.random((B, H, W, NC)) * (np.random.random((B, H, W, NC)) > 0.25)),
            "conv_w": bf(np.random.uniform(-lim, lim, (CH, 3, 3, DIM)) / s[:, None, None, None])}


def reference(x, seg_mask, conv_w):
    x, seg_mask, conv_w = f64(x), f64(seg_mask), f64(conv_w)
    s_patch = _patches3x3(seg_mask)
    m = seg_mask[:, :, :, None, :]
    s_max = np.max(m, axis=-1, keepdims=True)
    sel = np.sum(np.where(m == s_max, s_patch, 0.0), axis=-1)
    cnt = np.sum((sel != 0.0).astype(np.float64), axis=-1, keepdims=True)
    norm = np.where(cnt > 0, 9.0 / np.maximum(cnt, 1.0), 0.0)
    xp = _patches3x3(x)
    xp = xp * sel[..., None]
    w = conv_w.reshape(CH, 9, DIM)
    xq = mxq(xp.reshape(B * H * W, 9 * CH), 1, "e4m3")
    wq = mxq(w.transpose(1, 0, 2).reshape(9 * CH, DIM), 0, "e4m3")
    out = (xq @ wq).reshape(B, H, W, DIM) * norm
    return out

@@ -1,0 +1,281 @@
+from contextlib import ExitStack
+
+import concourse.mybir as mybir
+from concourse.masks import make_identity
+
+F32 = mybir.dt.float32
+BF16 = mybir.dt.bfloat16
+U32 = mybir.dt.uint32
+U8 = mybir.dt.uint8
+FP8X4 = mybir.dt.float8_e4m3fn_x4
+ALU = mybir.AluOpType
+ACTF = mybir.ActivationFunctionType
+AX = mybir.AxisListType
+
+P = 128
+NCLS = 22
+TAPS = 9
+DIM = 512
+FLOPS = 2 * 1024 * 4608 * 512
+
+PINNED = True
+W_ON_VECTOR = (2, 5, 8)
+FILL = (6, 12, 16, 16, 16, 16, 16)
+VPARTS = 1
+
+
+def tile_partialconvolution_kernel(tc, x, seg_mask, conv_w, out):
+    nc = tc.nc
+    xv = x.rearrange("b h w (t c) -> (b h w t) c", t=4).rearrange("(n q) c -> q n c", q=P)
+    sv = seg_mask.rearrange("b h w c -> (b h w) c").rearrange("(m p) c -> p m c", p=P)
+    wv = conv_w.rearrange("(t p) i j d -> p t (i j) d", p=P)
+    ov = out.rearrange("b h w d -> (b h w) d")
+
+    with ExitStack() as ctx:
+        if PINNED:
+            ctx.enter_context(tc.manual_schedule())
+        const = ctx.enter_context(tc.tile_pool(name="const", bufs=1))
+        gpool = ctx.enter_context(tc.tile_pool(name="gated", bufs=12))
+        wgpool = ctx.enter_context(tc.tile_pool(name="wgrouped", bufs=9))
+        xqpool = ctx.enter_context(tc.tile_pool(name="xquant", bufs=3))
+        rpool = ctx.enter_context(tc.tile_pool(name="result", bufs=4))
+        psum = ctx.enter_context(tc.psum_pool(name="psum", bufs=4))
+
+        m0 = const.tile([P, 8, NCLS], BF16, name="m0")
+        xs = const.tile([P, 32, P], BF16, name="xs")
+        wraw = const.tile([P, 4, TAPS, DIM], BF16, name="wraw")
+
+        def load_w(k):
+            nc.sync.dma_start(out=wraw[:, :, k, :], in_=wv[:, :, k, :])
+
+        def load_x(ip):
+            nc.sync.dma_start(out=xs[:, 16 * ip : 16 * ip + 16, :], in_=xv[:, 16 * ip : 16 * ip + 16, :])
+
+        nc.sync.dma_start(out=m0[:], in_=sv)
+        load_w(0)
+        load_x(0)
+        for k in range(1, TAPS):
+            load_w(k)
+        load_x(1)
+
+        ident = const.tile([P, P], BF16, name="ident")
+        make_identity(nc, ident[:])
+        wide = const.tile([P, 3, 384], BF16, name="wide")
+        nc.vector.memset(wide[:], 0.0)
+        gq = [const.tile([P, 6, 1024], BF16, name="gq%d" % tg, align_bytes=64) for tg in range(3)]
+        nc.vector.memset(gq[0][:, :, 0:80], 0.0)
+        nc.vector.memset(gq[1][:, :, 0:16], 0.0)
+        nc.vector.memset(gq[1][:, :, 1008:1024], 0.0)
+        nc.vector.memset(gq[2][:, :, 944:1024], 0.0)
+        nc.vector.tensor_copy(out=wide[:, :, 128:256], in_=ident[:].unsqueeze(1).to_broadcast([P, 3, P]))
+        w16 = wide[:, :, 128:256].rearrange("p j (a b) -> p j a b", b=16)
+        nc.vector.memset(w16[:, 0, :, 0:1], 0.0)
+        nc.vector.memset(w16[:, 2, :, 15:16], 0.0)
+        rrep = const.tile([P, P, 4], F32, name="rrep")
+        nc.vector.tensor_copy(out=rrep[:], in_=ident[:].unsqueeze(2).to_broadcast([P, P, 4]))
+
+        mx0 = const.tile([P, 8], F32, name="mx0")
+        e0 = const.tile([P, 8, NCLS], BF16, name="e0")
+        prod = const.tile([P, 2, TAPS, 4, NCLS], BF16, name="prod")
+        sels = const.tile([P, 2, TAPS, 4], F32, name="sels")
+        nz = const.tile([P, 2, TAPS, 4], BF16, name="nz")
+        selr = const.tile([P, 2, 4, TAPS * 4], F32, name="selr")
+        cmax = const.tile([P, 8], F32, name="cmax")
+        crec = const.tile([P, 8], F32, name="crec")
+        norm = const.tile([P, 8], F32, name="norm")
+
+        nc.vector.tensor_reduce(out=mx0[:], in_=m0[:], axis=AX.X, op=ALU.max)
+        nc.vector.tensor_tensor(
+            out=e0[:], in0=m0[:], in1=mx0[:].unsqueeze(2).to_broadcast([P, 8, NCLS]), op=ALU.is_equal
+        )
+
+        cps = []
+
+        def shift_onehot(ip, tg):
+            esh = psum.tile([P, 3, 4, NCLS], F32, name="esh", tag=("tp" if ip == 0 else "acc"))
+            di = tg - 1
+            for kk in range(3):
+                sh = 16 * di + kk - 1
+                nc.tensor.matmul(
+                    out=esh[:, kk, :, :],
+                    lhsT=wide[:, kk, 128 - sh : 256 - sh],
+                    rhs=e0[:, 4 * ip : 4 * ip + 4, :],
+                    start=True,
+                    stop=(di == 0),
+                )
+                if di == 1:
+                    nc.tensor.matmul(
+                        out=esh[:, kk, 1:4:2, :],
+                        lhsT=wide[:, kk, 256 - sh : 384 - sh],
+                        rhs=e0[:, 4 * ip : 4 * ip + 4 : 2, :],
+                        start=False,
+                        stop=True,
+                    )
+                if di == -1:
+                    nc.tensor.matmul(
+                        out=esh[:, kk, 0:4:2, :],
+                        lhsT=wide[:, kk, -sh : 128 - sh],
+                        rhs=e0[:, 4 * ip + 1 : 4 * ip + 4 : 2, :],
+                        start=False,
+                        stop=True,
+                    )
+            return esh
+
+        def dot_classes(ip, tg, esh):
+            ks = slice(3 * tg, 3 * tg + 3)
+            nc.vector.tensor_tensor(
+                out=prod[:, ip, ks, :, :],
+                in0=esh[:],
+                in1=m0[:, 4 * ip : 4 * ip + 4, :].unsqueeze(1).to_broadcast([P, 3, 4, NCLS]),
+                op=ALU.mult,
+            )
+            nc.vector.tensor_reduce(out=sels[:, ip, ks, :], in_=prod[:, ip, ks, :, :], axis=AX.X, op=ALU.add)
+
+        def replicate(ip):
+            rp = psum.tile([P, 4, TAPS * 4], F32, name="rp", tag=("tp" if ip == 0 else "acc"))
+            for g in range(4):
+                nc.tensor.matmul(
+                    out=rp[:, g, :],
+                    lhsT=rrep[:, 32 * g : 32 * g + 32, :].rearrange("p a t -> p (a t)"),
+                    rhs=sels[:, ip, :, :].rearrange("p k m -> p (k m)"),
+                    start=True,
+                    stop=True,
+                )
+            return rp
+
+        def count_taps():
+            nc.vector.tensor_single_scalar(out=nz[:], in_=sels[:], scalar=0.0, op=ALU.not_equal)
+            cp = psum.tile([P, 2, 4], F32, name="cp", tag="acc")
+            cps.append(cp)
+            steps = []
+            for k in range(TAPS):
+                di = k // 3 - 1
+                sh = 16 * di + k % 3 - 1
+                steps.append((cp[:, :, :], 128 + sh, nz[:, :, k, :]))
+                if di == 1:
+                    steps.append((cp[:, :, 0:4:2], sh, nz[:, :, k, 1:4:2]))
+                if di == -1:
+                    steps.append((cp[:, :, 1:4:2], 256 + sh, nz[:, :, k, 0:4:2]))
+            for i, (o, c0, r) in enumerate(steps):
+                nc.tensor.matmul(
+                    out=o, lhsT=wide[:, 1, c0 : c0 + P], rhs=r, start=(i == 0), stop=(i == len(steps) - 1)
+                )
+
+        def make_norm():
+            cp = cps[0]
+            nc.vector.tensor_scalar_max(out=cmax[:], in0=cp[:].rearrange("p a b -> p (a b)"), scalar1=1.0)
+            nc.vector.reciprocal(out=crec[:], in_=cmax[:])
+            nc.vector.tensor_scalar_mul(out=norm[:], in0=crec[:], scalar1=9.0)
+
+        wq = const.tile([P, TAPS, DIM], U32, name="wq", align_bytes=64)
+        ws = const.tile([P, TAPS, DIM], U8, name="ws", align_bytes=64)
+        wg = {}
+
+        def regroup_w(k, part, parts):
+            if part == 0:
+                wg[k] = wgpool.tile([P, DIM, 4], BF16, name="wg", tag="wg", align_bytes=64)
+            n = DIM // parts
+            dst = wg[k][:, part * n : (part + 1) * n, :].rearrange("p (c i) t -> p c t i", i=4)
+            src = wraw[:, :, k, part * n : (part + 1) * n].rearrange("p t (c i) -> p c t i", i=4)
+            if k in W_ON_VECTOR:
+                nc.vector.tensor_copy(out=dst, in_=src)
+            else:
+                nc.scalar.copy(out=dst, in_=src)
+
+        def quantise_w(k):
+            nc.vector.quantize_mx(
+                out=wq[:, k, :].bitcast(FP8X4), scales=ws[:, k, :], in_=wg[k][:].rearrange("p d t -> p (d t)")
+            )
+
+        xq = {}
+        xsc = {}
+        acc = {}
+
+        def prepare(g, fill=()):
+            fill = list(fill)
+            ip, tg = g // 3, g % 3
+            for u in range(6):
+                il, kk = u // 3, u % 3
+                b, k = 2 * ip + il, 3 * tg + kk
+                sh = 16 * (tg - 1) + kk - 1
+                gt = gpool.tile([P, 8, P], BF16, name="gt", tag="gt")
+                for nn in range(8):
+                    n = 8 * b + nn
+                    col = 4 * k + (n // 4) % 4
+                    nc.vector.tensor_scalar_mul(
+                        out=gt[:, nn, :], in0=xs[:, n, :], scalar1=selr[:, ip, n % 4, col : col + 1]
+                    )
+                pst = psum.tile([P, 1024], BF16, name="pst", tag="tp")
+                for nn in range(8):
+                    nc.tensor.transpose(out=pst[:, nn * P : (nn + 1) * P], in_=gt[:, nn, :], identity=ident[:])
+                d0, d1 = max(0, -sh), min(256, 256 - sh)
+                nc.scalar.copy(out=gq[tg][:, u, 4 * d0 : 4 * d1], in_=pst[:, 4 * (d0 + sh) : 4 * (d1 + sh)])
+                for f in fill[u * len(fill) // 6 : (u + 1) * len(fill) // 6]:
+                    regroup_w(f[0], f[1], 4)
+
+        def quantise_x(g):
+            tg = g % 3
+            xq[g] = xqpool.tile([P, 6, 256], U32, name="xq", tag="xq", align_bytes=64)
+            xsc[g] = xqpool.tile([P, 6, 256], U8, name="xsc", tag="xsc", align_bytes=64)
+            for u0, u1 in ((0, 4), (4, 6)):
+                nc.vector.quantize_mx(
+                    out=xq[g][:, u0:u1, :].rearrange("p u w -> p (u w)").bitcast(FP8X4),
+                    scales=xsc[g][:, u0:u1, :].rearrange("p u w -> p (u w)"),
+                    in_=gq[tg][:, u0:u1, :].rearrange("p u w -> p (u w)"),
+                )
+
+        def multiply(g):
+            ip, tg = g // 3, g % 3
+            for il in range(2):
+                for mm in range(2):
+                    if tg == 0:
+                        acc[(il, mm)] = psum.tile([P, DIM], F32, name="acc", tag="acc")
+                    for kk in range(3):
+                        u, k = 3 * il + kk, 3 * tg + kk
+                        nc.tensor.matmul_mx(
+                            out=acc[(il, mm)][:],
+                            lhsT=xq[g][:, u, mm * P : (mm + 1) * P].bitcast(FP8X4),
+                            lhsT_scale=xsc[g][:, u, mm * P : (mm + 1) * P],
+                            rhs=wq[:, k, :].bitcast(FP8X4),
+                            rhs_scale=ws[:, k, :],
+                            start=(k == 0),
+                            stop=(k == TAPS - 1),
+                        )
+                    if tg == 2:
+                        m = 4 * ip + 2 * il + mm
+                        res = rpool.tile([P, DIM], F32, name="res", tag="res")
+                        nc.scalar.activation(out=res[:], in_=acc[(il, mm)][:], func=ACTF.Copy, scale=norm[:, m : m + 1])
+                        nc.sync.dma_start(out=ov[m * P : (m + 1) * P, :], in_=res[:])
+
+        esh = {}
+        for ip in range(2):
+            for tg in range(3):
+                esh[(ip, tg)] = shift_onehot(ip, tg)
+        for k in (0, 1):
+            for part in range(4):
+                regroup_w(k, part, 4)
+        for tg in range(3):
+            dot_classes(0, tg, esh[(0, tg)])
+        rp0 = replicate(0)
+        dot_classes(1, 0, esh[(1, 0)])
+        dot_classes(1, 1, esh[(1, 1)])
+        nc.vector.tensor_copy(out=selr[:, 0], in_=rp0[:])
+        sfill = [(k, part) for k in (3, 4, 6, 7) for part in range(4)]
+        prepare(0, sfill[0:FILL[0]])
+        dot_classes(1, 2, esh[(1, 2)])
+        rp1 = replicate(1)
+        count_taps()
+        prepare(1, sfill[FILL[0]:FILL[1]])
+        nc.vector.tensor_copy(out=selr[:, 1], in_=rp1[:])
+        make_norm()
+        for g in range(6):
+            if g < 3:
+                for k in range(3 * g, 3 * g + 3):
+                    if k in W_ON_VECTOR:
+                        for part in range(VPARTS):
+                            regroup_w(k, part, VPARTS)
+                    quantise_w(k)
+            quantise_x(g)
+            multiply(g)
+            if g + 2 < 6:
+                prepare(g + 2, sfill[FILL[g + 1]:FILL[g + 2]])

@@ -42,14 +42,14 @@ def tile_partialconvolution_kernel(tc, x, seg_mask, conv_w, out):
         psum = ctx.enter_context(tc.psum_pool(name="psum", bufs=4))
 
         m0 = const.tile([P, 8, NCLS], BF16, name="m0")
-        xs = const.tile([P, 32, P], BF16, name="xs")
-        wraw = const.tile([P, 4, TAPS, DIM], BF16, name="wraw")
+        xs = [const.tile([P, 16, P], BF16, name="xs%d" % ip) for ip in range(2)]
+        wraw = [const.tile([P, 4, DIM], BF16, name="wraw%d" % k) for k in range(TAPS)]
 
         def load_w(k):
-            nc.sync.dma_start(out=wraw[:, :, k, :], in_=wv[:, :, k, :])
+            nc.sync.dma_start(out=wraw[k][:], in_=wv[:, :, k, :])
 
         def load_x(ip):
-            nc.sync.dma_start(out=xs[:, 16 * ip : 16 * ip + 16, :], in_=xv[:, 16 * ip : 16 * ip + 16, :])
+            nc.sync.dma_start(out=xs[ip][:], in_=xv[:, 16 * ip : 16 * ip + 16, :])
 
         nc.sync.dma_start(out=m0[:], in_=sv)
         load_w(0)
@@ -176,7 +176,7 @@ def tile_partialconvolution_kernel(tc, x, seg_mask, conv_w, out):
                 wg[k] = wgpool.tile([P, DIM, 4], BF16, name="wg", tag="wg", align_bytes=64)
             n = DIM // parts
             dst = wg[k][:, part * n : (part + 1) * n, :].rearrange("p (c i) t -> p c t i", i=4)
-            src = wraw[:, :, k, part * n : (part + 1) * n].rearrange("p t (c i) -> p c t i", i=4)
+            src = wraw[k][:, :, part * n : (part + 1) * n].rearrange("p t (c i) -> p c t i", i=4)
             if k in W_ON_VECTOR:
                 nc.vector.tensor_copy(out=dst, in_=src)
             else:
@@ -203,7 +203,7 @@ def tile_partialconvolution_kernel(tc, x, seg_mask, conv_w, out):
                     n = 8 * b + nn
                     col = 4 * k + (n // 4) % 4
                     nc.vector.tensor_scalar_mul(
-                        out=gt[:, nn, :], in0=xs[:, n, :], scalar1=selr[:, ip, n % 4, col : col + 1]
+                        out=gt[:, nn, :], in0=xs[ip][:, n % 16, :], scalar1=selr[:, ip, n % 4, col : col + 1]
                     )
                 pst = psum.tile([P, 1024], BF16, name="pst", tag="tp")
                 for nn in range(8):

@@ -20,8 +20,15 @@ FLOPS = 2 * 1024 * 4608 * 512
 
 PINNED = True
 W_ON_VECTOR = (2, 5, 8)
+W_ON_GPSIMD = ()
+S_HEAD = (0, 1)
+S_FILL = (3, 4, 6, 7)
+LOADS = (0, -1, 1, 2, 3, 4, 5, 6, 7, 8, -2)
 FILL = (6, 12, 16, 16, 16, 16, 16)
 VPARTS = 1
+WARM0 = 6
+WARM1 = 2
+SUST = 2
 
 
 def tile_partialconvolution_kernel(tc, x, seg_mask, conv_w, out):
@@ -52,12 +59,21 @@ def tile_partialconvolution_kernel(tc, x, seg_mask, conv_w, out):
             nc.sync.dma_start(out=xs[ip][:], in_=xv[:, 16 * ip : 16 * ip + 16, :])
 
         nc.sync.dma_start(out=m0[:], in_=sv)
-        load_w(0)
-        load_x(0)
-        for k in range(1, TAPS):
-            load_w(k)
-        load_x(1)
+        for item in LOADS:
+            if item < 0:
+                load_x(-item - 1)
+            else:
+                load_w(item)
 
+        zeros = const.tile([P, DIM], BF16, name="zeros")
+        nc.vector.memset(zeros[:], 0.0)
+
+        def warm(dst, times):
+            for i in range(times):
+                nc.tensor.matmul(out=dst, lhsT=zeros[:, 0:P], rhs=zeros[:], start=True, stop=True)
+
+        warmt = psum.tile([P, DIM], F32, name="warmt", tag="tp")
+        warm(warmt[:], WARM0)
         ident = const.tile([P, P], BF16, name="ident")
         make_identity(nc, ident[:])
         wide = const.tile([P, 3, 384], BF16, name="wide")
@@ -179,6 +195,8 @@ def tile_partialconvolution_kernel(tc, x, seg_mask, conv_w, out):
             src = wraw[k][:, :, part * n : (part + 1) * n].rearrange("p t (c i) -> p c t i", i=4)
             if k in W_ON_VECTOR:
                 nc.vector.tensor_copy(out=dst, in_=src)
+            elif k in W_ON_GPSIMD:
+                nc.gpsimd.tensor_scalar(out=dst, in0=src, scalar1=1.0, scalar2=0.0, op0=ALU.mult, op1=ALU.add)
             else:
                 nc.scalar.copy(out=dst, in_=src)
 
@@ -206,6 +224,8 @@ def tile_partialconvolution_kernel(tc, x, seg_mask, conv_w, out):
                         out=gt[:, nn, :], in0=xs[ip][:, n % 16, :], scalar1=selr[:, ip, n % 4, col : col + 1]
                     )
                 pst = psum.tile([P, 1024], BF16, name="pst", tag="tp")
+                if g < 2 and u % SUST == 0:
+                    warm(pst[:, 0:DIM], 1)
                 for nn in range(8):
                     nc.tensor.transpose(out=pst[:, nn * P : (nn + 1) * P], in_=gt[:, nn, :], identity=ident[:])
                 d0, d1 = max(0, -sh), min(256, 256 - sh)
@@ -251,7 +271,10 @@ def tile_partialconvolution_kernel(tc, x, seg_mask, conv_w, out):
         for ip in range(2):
             for tg in range(3):
                 esh[(ip, tg)] = shift_onehot(ip, tg)
-        for k in (0, 1):
+        warm(warmt[:], WARM1)
+        for k in W_ON_GPSIMD:
+            regroup_w(k, 0, 1)
+        for k in S_HEAD:
             for part in range(4):
                 regroup_w(k, part, 4)
         for tg in range(3):
@@ -260,7 +283,7 @@ def tile_partialconvolution_kernel(tc, x, seg_mask, conv_w, out):
         dot_classes(1, 0, esh[(1, 0)])
         dot_classes(1, 1, esh[(1, 1)])
         nc.vector.tensor_copy(out=selr[:, 0], in_=rp0[:])
-        sfill = [(k, part) for k in (3, 4, 6, 7) for part in range(4)]
+        sfill = [(k, part) for k in S_FILL for part in range(4)]
         prepare(0, sfill[0:FILL[0]])
         dot_classes(1, 2, esh[(1, 2)])
         rp1 = replicate(1)

@@ -19,23 +19,29 @@ DIM = 512
 FLOPS = 2 * 1024 * 4608 * 512
 
 PINNED = True
-W_ON_VECTOR = (2, 5, 8)
+W_ON_VECTOR = (2, 4, 5, 7, 8)
 W_ON_GPSIMD = ()
 S_HEAD = (0, 1)
-S_FILL = (3, 4, 6, 7)
+S_FILL = (3, 6)
 LOADS = (0, -1, 1, 2, 3, 4, 5, 6, 7, 8, -2)
-FILL = (6, 12, 16, 16, 16, 16, 16)
+FILL = (0, 4, 8, 8, 8, 8, 8)
 VPARTS = 1
 WARM0 = 6
 WARM1 = 2
-SUST = 2
+SUST = 3
+SUSTW = 512
+SPLIT_R = False
+APATH = False
+RAWAT = 1
+CNTAT = 1
+NDOT_EARLY = 1
 
 
 def tile_partialconvolution_kernel(tc, x, seg_mask, conv_w, out):
     nc = tc.nc
-    xv = x.rearrange("b h w (t c) -> (b h w t) c", t=4).rearrange("(n q) c -> q n c", q=P)
+    xv = x.rearrange("b h w (t c) -> (b h w t) c", t=2).rearrange("(n q) c -> q n c", q=P)
     sv = seg_mask.rearrange("b h w c -> (b h w) c").rearrange("(m p) c -> p m c", p=P)
-    wv = conv_w.rearrange("(t p) i j d -> p t (i j) d", p=P)
+    wv = conv_w.rearrange("(t u p) i j d -> p u t (i j) d", t=2, u=2, p=P)
     ov = out.rearrange("b h w d -> (b h w) d")
 
     with ExitStack() as ctx:
@@ -49,14 +55,15 @@ def tile_partialconvolution_kernel(tc, x, seg_mask, conv_w, out):
         psum = ctx.enter_context(tc.psum_pool(name="psum", bufs=4))
 
         m0 = const.tile([P, 8, NCLS], BF16, name="m0")
-        xs = [const.tile([P, 16, P], BF16, name="xs%d" % ip) for ip in range(2)]
+        xs = [const.tile([P, 8, 256], BF16, name="xs%d" % ip) for ip in range(2)]
         wraw = [const.tile([P, 4, DIM], BF16, name="wraw%d" % k) for k in range(TAPS)]
 
         def load_w(k):
-            nc.sync.dma_start(out=wraw[k][:], in_=wv[:, :, k, :])
+            for u in range(2):
+                nc.sync.dma_start(out=wraw[k][:, 2 * u : 2 * u + 2, :], in_=wv[:, u, :, k, :])
 
         def load_x(ip):
-            nc.sync.dma_start(out=xs[ip][:], in_=xv[:, 16 * ip : 16 * ip + 16, :])
+            nc.sync.dma_start(out=xs[ip][:], in_=xv[:, 8 * ip : 8 * ip + 8, :])
 
         nc.sync.dma_start(out=m0[:], in_=sv)
         for item in LOADS:
@@ -68,9 +75,9 @@ def tile_partialconvolution_kernel(tc, x, seg_mask, conv_w, out):
         zeros = const.tile([P, DIM], BF16, name="zeros")
         nc.vector.memset(zeros[:], 0.0)
 
-        def warm(dst, times):
+        def warm(dst, times, width=DIM):
             for i in range(times):
-                nc.tensor.matmul(out=dst, lhsT=zeros[:, 0:P], rhs=zeros[:], start=True, stop=True)
+                nc.tensor.matmul(out=dst, lhsT=zeros[:, 0:P], rhs=zeros[:, 0:width], start=True, stop=True)
 
         warmt = psum.tile([P, DIM], F32, name="warmt", tag="tp")
         warm(warmt[:], WARM0)
@@ -87,15 +94,25 @@ def tile_partialconvolution_kernel(tc, x, seg_mask, conv_w, out):
         w16 = wide[:, :, 128:256].rearrange("p j (a b) -> p j a b", b=16)
         nc.vector.memset(w16[:, 0, :, 0:1], 0.0)
         nc.vector.memset(w16[:, 2, :, 15:16], 0.0)
-        rrep = const.tile([P, P, 4], F32, name="rrep")
-        nc.vector.tensor_copy(out=rrep[:], in_=ident[:].unsqueeze(2).to_broadcast([P, P, 4]))
+        rrep = const.tile([P, P, 2], F32, name="rrep")
+        nc.vector.tensor_copy(out=rrep[:], in_=ident[:].unsqueeze(2).to_broadcast([P, P, 2]))
 
         mx0 = const.tile([P, 8], F32, name="mx0")
         e0 = const.tile([P, 8, NCLS], BF16, name="e0")
         prod = const.tile([P, 2, TAPS, 4, NCLS], BF16, name="prod")
-        sels = const.tile([P, 2, TAPS, 4], F32, name="sels")
+        selsp = const.tile([P, P], F32, name="selsp")
+        nc.vector.memset(selsp[:, 72:P], 0.0)
+        sels = selsp[:, 0:72].rearrange("p (i k m) -> p i k m", i=2, k=TAPS)
+        xt = []
+        if APATH:
+            identf = const.tile([P, P], F32, name="identf")
+            nc.vector.tensor_copy(out=identf[:], in_=ident[:])
+            selt = const.tile([P, P], F32, name="selt")
+            selb = const.tile([P, 12 * P], F32, name="selb")
+            xt = [const.tile([P, 1024], BF16, name="xt%d" % il) for il in range(2)]
+            scratch = ov[992:1024, :].rearrange("a (b c) -> (a b) c", c=P)
         nz = const.tile([P, 2, TAPS, 4], BF16, name="nz")
-        selr = const.tile([P, 2, 4, TAPS * 4], F32, name="selr")
+        selr = const.tile([P, 2, 2 * TAPS * 4], F32, name="selr")
         cmax = const.tile([P, 8], F32, name="cmax")
         crec = const.tile([P, 8], F32, name="crec")
         norm = const.tile([P, 8], F32, name="norm")
@@ -147,17 +164,20 @@ def tile_partialconvolution_kernel(tc, x, seg_mask, conv_w, out):
             )
             nc.vector.tensor_reduce(out=sels[:, ip, ks, :], in_=prod[:, ip, ks, :, :], axis=AX.X, op=ALU.add)
 
-        def replicate(ip):
-            rp = psum.tile([P, 4, TAPS * 4], F32, name="rp", tag=("tp" if ip == 0 else "acc"))
-            for g in range(4):
+        def replicate(c0, c1, tag):
+            rp = psum.tile([P, 2, c1 - c0], F32, name="rp", tag=tag)
+            for g in range(2):
                 nc.tensor.matmul(
                     out=rp[:, g, :],
-                    lhsT=rrep[:, 32 * g : 32 * g + 32, :].rearrange("p a t -> p (a t)"),
-                    rhs=sels[:, ip, :, :].rearrange("p k m -> p (k m)"),
+                    lhsT=rrep[:, 64 * g : 64 * g + 64, :].rearrange("p a t -> p (a t)"),
+                    rhs=selsp[:, c0:c1],
                     start=True,
                     stop=True,
                 )
             return rp
+
+        def keep_gate(rp, c0, c1):
+            nc.vector.tensor_copy(out=selr[:, :, c0:c1], in_=rp[:])
 
         def count_taps():
             nc.vector.tensor_single_scalar(out=nz[:], in_=sels[:], scalar=0.0, op=ALU.not_equal)
@@ -209,6 +229,16 @@ def tile_partialconvolution_kernel(tc, x, seg_mask, conv_w, out):
         xsc = {}
         acc = {}
 
+        def transpose_unit(pst, src):
+            words = pst[:].rearrange("p (s f) -> p s f", f=4)
+            for nn in range(4):
+                for u in range(2):
+                    nc.tensor.transpose(
+                        out=words[:, 64 * nn : 64 * nn + 64, 2 * u : 2 * u + 2],
+                        in_=src[:, nn, u * P : (u + 1) * P],
+                        identity=ident[:],
+                    )
+
         def prepare(g, fill=()):
             fill = list(fill)
             ip, tg = g // 3, g % 3
@@ -216,22 +246,47 @@ def tile_partialconvolution_kernel(tc, x, seg_mask, conv_w, out):
                 il, kk = u // 3, u % 3
                 b, k = 2 * ip + il, 3 * tg + kk
                 sh = 16 * (tg - 1) + kk - 1
-                gt = gpool.tile([P, 8, P], BF16, name="gt", tag="gt")
-                for nn in range(8):
-                    n = 8 * b + nn
-                    col = 4 * k + (n // 4) % 4
+                gt = gpool.tile([P, 4, 256], BF16, name="gt", tag="gt")
+                for nn in range(4):
+                    n = 4 * b + nn
+                    col = 36 * ip + 4 * k + (n // 2) % 4
                     nc.vector.tensor_scalar_mul(
-                        out=gt[:, nn, :], in0=xs[ip][:, n % 16, :], scalar1=selr[:, ip, n % 4, col : col + 1]
+                        out=gt[:, nn, :], in0=xs[ip][:, n % 8, :], scalar1=selr[:, n % 2, col : col + 1]
                     )
                 pst = psum.tile([P, 1024], BF16, name="pst", tag="tp")
                 if g < 2 and u % SUST == 0:
-                    warm(pst[:, 0:DIM], 1)
-                for nn in range(8):
-                    nc.tensor.transpose(out=pst[:, nn * P : (nn + 1) * P], in_=gt[:, nn, :], identity=ident[:])
+                    warm(pst[:, 0:SUSTW], 1, SUSTW)
+                transpose_unit(pst, gt)
                 d0, d1 = max(0, -sh), min(256, 256 - sh)
                 nc.scalar.copy(out=gq[tg][:, u, 4 * d0 : 4 * d1], in_=pst[:, 4 * (d0 + sh) : 4 * (d1 + sh)])
                 for f in fill[u * len(fill) // 6 : (u + 1) * len(fill) // 6]:
                     regroup_w(f[0], f[1], 4)
+
+        def spread_gate():
+            tp = psum.tile([P, P], F32, name="tp", tag="acc")
+            nc.tensor.transpose(out=tp[:], in_=selsp[:], identity=identf[:])
+            nc.scalar.copy(out=selt[:], in_=tp[:])
+            nc.sync.dma_start(out=scratch, in_=selt[:])
+            nc.sync.dma_start(out=selb[:], in_=scratch[60:72, :].rearrange("r c -> (r c)").partition_broadcast(P))
+
+        def transpose_raw(il):
+            pst = psum.tile([P, 1024], BF16, name="pst", tag="tp")
+            transpose_unit(pst, xs[1][:, 4 * il : 4 * il + 4, :])
+            nc.scalar.copy(out=xt[il][:], in_=pst[:])
+
+        def prepare_late(g):
+            tg = g % 3
+            for u in range(6):
+                il, kk = u // 3, u % 3
+                sh = 16 * (tg - 1) + kk - 1
+                n = 256 - sh
+                c0 = 512 * kk + 256 * il + sh
+                nc.vector.tensor_tensor(
+                    out=gq[tg][:, u, 0 : 4 * n].rearrange("p (s t) -> p s t", t=4),
+                    in0=xt[il][:, 4 * sh : 1024].rearrange("p (s t) -> p s t", t=4),
+                    in1=selb[:, c0 : c0 + n].unsqueeze(2).to_broadcast([P, n, 4]),
+                    op=ALU.mult,
+                )
 
         def quantise_x(g):
             tg = g % 3
@@ -277,20 +332,39 @@ def tile_partialconvolution_kernel(tc, x, seg_mask, conv_w, out):
         for k in S_HEAD:
             for part in range(4):
                 regroup_w(k, part, 4)
-        for tg in range(3):
-            dot_classes(0, tg, esh[(0, tg)])
-        rp0 = replicate(0)
-        dot_classes(1, 0, esh[(1, 0)])
-        dot_classes(1, 1, esh[(1, 1)])
-        nc.vector.tensor_copy(out=selr[:, 0], in_=rp0[:])
         sfill = [(k, part) for k in S_FILL for part in range(4)]
-        prepare(0, sfill[0:FILL[0]])
-        dot_classes(1, 2, esh[(1, 2)])
-        rp1 = replicate(1)
-        count_taps()
-        prepare(1, sfill[FILL[0]:FILL[1]])
-        nc.vector.tensor_copy(out=selr[:, 1], in_=rp1[:])
-        make_norm()
+        if SPLIT_R:
+            dot_classes(0, 0, esh[(0, 0)])
+            rpa = replicate(0, 12, "tp")
+            dot_classes(0, 1, esh[(0, 1)])
+            dot_classes(0, 2, esh[(0, 2)])
+            for tg in range(NDOT_EARLY):
+                dot_classes(1, tg, esh[(1, tg)])
+            keep_gate(rpa, 0, 12)
+            if NDOT_EARLY == 3:
+                rpb = replicate(12, 72, "acc")
+                count_taps()
+            prepare(0, sfill[0:FILL[0]])
+            for tg in range(NDOT_EARLY, 3):
+                dot_classes(1, tg, esh[(1, tg)])
+            if NDOT_EARLY < 3:
+                rpb = replicate(12, 72, "acc")
+                count_taps()
+            keep_gate(rpb, 12, 72)
+            prepare(1, sfill[FILL[0]:FILL[1]])
+            make_norm()
+        else:
+            for tg in range(3):
+                dot_classes(0, tg, esh[(0, tg)])
+            rp0 = replicate(0, 36, "tp")
+            dot_classes(1, 0, esh[(1, 0)])
+            dot_classes(1, 1, esh[(1, 1)])
+            keep_gate(rp0, 0, 36)
+            prepare(0, sfill[0:FILL[0]])
+            dot_classes(1, 2, esh[(1, 2)])
+            prepare(1, sfill[FILL[0]:FILL[1]])
+            rp1 = replicate(36, 72, "acc")
+            count_taps()
         for g in range(6):
             if g < 3:
                 for k in range(3 * g, 3 * g + 3):
@@ -299,6 +373,16 @@ def tile_partialconvolution_kernel(tc, x, seg_mask, conv_w, out):
                             regroup_w(k, part, VPARTS)
                     quantise_w(k)
             quantise_x(g)
+            if g == 0:
+                keep_gate(rp1, 36, 72)
+                make_norm()
+                if APATH:
+                    spread_gate()
             multiply(g)
-            if g + 2 < 6:
+            if APATH and g == RAWAT:
+                transpose_raw(0)
+                transpose_raw(1)
+            if APATH and g + 2 == 5:
+                prepare_late(5)
+            elif g + 2 < 6:
                 prepare(g + 2, sfill[FILL[g + 1]:FILL[g + 2]])

@@ -19,29 +19,27 @@ DIM = 512
 FLOPS = 2 * 1024 * 4608 * 512
 
 PINNED = True
-W_ON_VECTOR = (2, 4, 5, 7, 8)
+W_ON_VECTOR = (2, 5, 8)
 W_ON_GPSIMD = ()
 S_HEAD = (0, 1)
-S_FILL = (3, 6)
+S_FILL = (3, 4, 6, 7)
 LOADS = (0, -1, 1, 2, 3, 4, 5, 6, 7, 8, -2)
-FILL = (0, 4, 8, 8, 8, 8, 8)
+FILL = (6, 12, 16, 16, 16, 16, 16)
 VPARTS = 1
 WARM0 = 6
 WARM1 = 2
-SUST = 3
+SUST = 2
 SUSTW = 512
 SPLIT_R = False
-APATH = False
-RAWAT = 1
-CNTAT = 1
+TAPMAJOR = True
 NDOT_EARLY = 1
 
 
 def tile_partialconvolution_kernel(tc, x, seg_mask, conv_w, out):
     nc = tc.nc
-    xv = x.rearrange("b h w (t c) -> (b h w t) c", t=2).rearrange("(n q) c -> q n c", q=P)
+    xv = x.rearrange("b h w (t c) -> (b h w t) c", t=4).rearrange("(n q) c -> q n c", q=P)
     sv = seg_mask.rearrange("b h w c -> (b h w) c").rearrange("(m p) c -> p m c", p=P)
-    wv = conv_w.rearrange("(t u p) i j d -> p u t (i j) d", t=2, u=2, p=P)
+    wv = conv_w.rearrange("(t p) i j d -> p t (i j) d", p=P)
     ov = out.rearrange("b h w d -> (b h w) d")
 
     with ExitStack() as ctx:
@@ -55,15 +53,14 @@ def tile_partialconvolution_kernel(tc, x, seg_mask, conv_w, out):
         psum = ctx.enter_context(tc.psum_pool(name="psum", bufs=4))
 
         m0 = const.tile([P, 8, NCLS], BF16, name="m0")
-        xs = [const.tile([P, 8, 256], BF16, name="xs%d" % ip) for ip in range(2)]
+        xs = [const.tile([P, 16, P], BF16, name="xs%d" % ip) for ip in range(2)]
         wraw = [const.tile([P, 4, DIM], BF16, name="wraw%d" % k) for k in range(TAPS)]
 
         def load_w(k):
-            for u in range(2):
-                nc.sync.dma_start(out=wraw[k][:, 2 * u : 2 * u + 2, :], in_=wv[:, u, :, k, :])
+            nc.sync.dma_start(out=wraw[k][:], in_=wv[:, :, k, :])
 
         def load_x(ip):
-            nc.sync.dma_start(out=xs[ip][:], in_=xv[:, 8 * ip : 8 * ip + 8, :])
+            nc.sync.dma_start(out=xs[ip][:], in_=xv[:, 16 * ip : 16 * ip + 16, :])
 
         nc.sync.dma_start(out=m0[:], in_=sv)
         for item in LOADS:
@@ -94,25 +91,15 @@ def tile_partialconvolution_kernel(tc, x, seg_mask, conv_w, out):
         w16 = wide[:, :, 128:256].rearrange("p j (a b) -> p j a b", b=16)
         nc.vector.memset(w16[:, 0, :, 0:1], 0.0)
         nc.vector.memset(w16[:, 2, :, 15:16], 0.0)
-        rrep = const.tile([P, P, 2], F32, name="rrep")
-        nc.vector.tensor_copy(out=rrep[:], in_=ident[:].unsqueeze(2).to_broadcast([P, P, 2]))
+        rrep = const.tile([P, P, 4], F32, name="rrep")
+        nc.vector.tensor_copy(out=rrep[:], in_=ident[:].unsqueeze(2).to_broadcast([P, P, 4]))
 
         mx0 = const.tile([P, 8], F32, name="mx0")
         e0 = const.tile([P, 8, NCLS], BF16, name="e0")
         prod = const.tile([P, 2, TAPS, 4, NCLS], BF16, name="prod")
-        selsp = const.tile([P, P], F32, name="selsp")
-        nc.vector.memset(selsp[:, 72:P], 0.0)
-        sels = selsp[:, 0:72].rearrange("p (i k m) -> p i k m", i=2, k=TAPS)
-        xt = []
-        if APATH:
-            identf = const.tile([P, P], F32, name="identf")
-            nc.vector.tensor_copy(out=identf[:], in_=ident[:])
-            selt = const.tile([P, P], F32, name="selt")
-            selb = const.tile([P, 12 * P], F32, name="selb")
-            xt = [const.tile([P, 1024], BF16, name="xt%d" % il) for il in range(2)]
-            scratch = ov[992:1024, :].rearrange("a (b c) -> (a b) c", c=P)
+        sels = const.tile([P, 2, TAPS, 4], F32, name="sels")
         nz = const.tile([P, 2, TAPS, 4], BF16, name="nz")
-        selr = const.tile([P, 2, 2 * TAPS * 4], F32, name="selr")
+        selr = const.tile([P, 4, 2 * TAPS * 4], F32, name="selr")
         cmax = const.tile([P, 8], F32, name="cmax")
         crec = const.tile([P, 8], F32, name="crec")
         norm = const.tile([P, 8], F32, name="norm")
@@ -165,12 +152,12 @@ def tile_partialconvolution_kernel(tc, x, seg_mask, conv_w, out):
             nc.vector.tensor_reduce(out=sels[:, ip, ks, :], in_=prod[:, ip, ks, :, :], axis=AX.X, op=ALU.add)
 
         def replicate(c0, c1, tag):
-            rp = psum.tile([P, 2, c1 - c0], F32, name="rp", tag=tag)
-            for g in range(2):
+            rp = psum.tile([P, 4, c1 - c0], F32, name="rp", tag=tag)
+            for g in range(4):
                 nc.tensor.matmul(
                     out=rp[:, g, :],
-                    lhsT=rrep[:, 64 * g : 64 * g + 64, :].rearrange("p a t -> p (a t)"),
-                    rhs=selsp[:, c0:c1],
+                    lhsT=rrep[:, 32 * g : 32 * g + 32, :].rearrange("p a t -> p (a t)"),
+                    rhs=sels[:].rearrange("p i k m -> p (i k m)")[:, c0:c1],
                     start=True,
                     stop=True,
                 )
@@ -229,16 +216,6 @@ def tile_partialconvolution_kernel(tc, x, seg_mask, conv_w, out):
         xsc = {}
         acc = {}
 
-        def transpose_unit(pst, src):
-            words = pst[:].rearrange("p (s f) -> p s f", f=4)
-            for nn in range(4):
-                for u in range(2):
-                    nc.tensor.transpose(
-                        out=words[:, 64 * nn : 64 * nn + 64, 2 * u : 2 * u + 2],
-                        in_=src[:, nn, u * P : (u + 1) * P],
-                        identity=ident[:],
-                    )
-
         def prepare(g, fill=()):
             fill = list(fill)
             ip, tg = g // 3, g % 3
@@ -246,58 +223,57 @@ def tile_partialconvolution_kernel(tc, x, seg_mask, conv_w, out):
                 il, kk = u // 3, u % 3
                 b, k = 2 * ip + il, 3 * tg + kk
                 sh = 16 * (tg - 1) + kk - 1
-                gt = gpool.tile([P, 4, 256], BF16, name="gt", tag="gt")
-                for nn in range(4):
-                    n = 4 * b + nn
-                    col = 36 * ip + 4 * k + (n // 2) % 4
+                gt = gpool.tile([P, 8, P], BF16, name="gt", tag="gt")
+                for nn in range(8):
+                    n = 8 * b + nn
+                    col = 36 * ip + 4 * k + (n // 4) % 4
                     nc.vector.tensor_scalar_mul(
-                        out=gt[:, nn, :], in0=xs[ip][:, n % 8, :], scalar1=selr[:, n % 2, col : col + 1]
+                        out=gt[:, nn, :], in0=xs[ip][:, n % 16, :], scalar1=selr[:, n % 4, col : col + 1]
                     )
                 pst = psum.tile([P, 1024], BF16, name="pst", tag="tp")
                 if g < 2 and u % SUST == 0:
                     warm(pst[:, 0:SUSTW], 1, SUSTW)
-                transpose_unit(pst, gt)
+                for nn in range(8):
+                    nc.tensor.transpose(out=pst[:, nn * P : (nn + 1) * P], in_=gt[:, nn, :], identity=ident[:])
                 d0, d1 = max(0, -sh), min(256, 256 - sh)
                 nc.scalar.copy(out=gq[tg][:, u, 4 * d0 : 4 * d1], in_=pst[:, 4 * (d0 + sh) : 4 * (d1 + sh)])
                 for f in fill[u * len(fill) // 6 : (u + 1) * len(fill) // 6]:
                     regroup_w(f[0], f[1], 4)
 
-        def spread_gate():
-            tp = psum.tile([P, P], F32, name="tp", tag="acc")
-            nc.tensor.transpose(out=tp[:], in_=selsp[:], identity=identf[:])
-            nc.scalar.copy(out=selt[:], in_=tp[:])
-            nc.sync.dma_start(out=scratch, in_=selt[:])
-            nc.sync.dma_start(out=selb[:], in_=scratch[60:72, :].rearrange("r c -> (r c)").partition_broadcast(P))
-
-        def transpose_raw(il):
-            pst = psum.tile([P, 1024], BF16, name="pst", tag="tp")
-            transpose_unit(pst, xs[1][:, 4 * il : 4 * il + 4, :])
-            nc.scalar.copy(out=xt[il][:], in_=pst[:])
-
-        def prepare_late(g):
+        def quantise_x(g, halves=(0, 1)):
             tg = g % 3
-            for u in range(6):
-                il, kk = u // 3, u % 3
-                sh = 16 * (tg - 1) + kk - 1
-                n = 256 - sh
-                c0 = 512 * kk + 256 * il + sh
-                nc.vector.tensor_tensor(
-                    out=gq[tg][:, u, 0 : 4 * n].rearrange("p (s t) -> p s t", t=4),
-                    in0=xt[il][:, 4 * sh : 1024].rearrange("p (s t) -> p s t", t=4),
-                    in1=selb[:, c0 : c0 + n].unsqueeze(2).to_broadcast([P, n, 4]),
-                    op=ALU.mult,
-                )
-
-        def quantise_x(g):
-            tg = g % 3
-            xq[g] = xqpool.tile([P, 6, 256], U32, name="xq", tag="xq", align_bytes=64)
-            xsc[g] = xqpool.tile([P, 6, 256], U8, name="xsc", tag="xsc", align_bytes=64)
-            for u0, u1 in ((0, 4), (4, 6)):
+            if 0 in halves:
+                xq[g] = xqpool.tile([P, 6, 256], U32, name="xq", tag="xq", align_bytes=64)
+                xsc[g] = xqpool.tile([P, 6, 256], U8, name="xsc", tag="xsc", align_bytes=64)
+            for u0, u1 in [((0, 4), (4, 6))[h] for h in halves]:
                 nc.vector.quantize_mx(
                     out=xq[g][:, u0:u1, :].rearrange("p u w -> p (u w)").bitcast(FP8X4),
                     scales=xsc[g][:, u0:u1, :].rearrange("p u w -> p (u w)"),
                     in_=gq[tg][:, u0:u1, :].rearrange("p u w -> p (u w)"),
                 )
+
+        def multiply_taps(g, kks):
+            ip, tg = g // 3, g % 3
+            for kk in kks:
+                for il in range(2):
+                    for mm in range(2):
+                        if tg == 0 and kk == 0:
+                            acc[(il, mm)] = psum.tile([P, DIM], F32, name="acc", tag="acc")
+                        u, k = 3 * il + kk, 3 * tg + kk
+                        nc.tensor.matmul_mx(
+                            out=acc[(il, mm)][:],
+                            lhsT=xq[g][:, u, mm * P : (mm + 1) * P].bitcast(FP8X4),
+                            lhsT_scale=xsc[g][:, u, mm * P : (mm + 1) * P],
+                            rhs=wq[:, k, :].bitcast(FP8X4),
+                            rhs_scale=ws[:, k, :],
+                            start=(k == 0),
+                            stop=(k == TAPS - 1),
+                        )
+                        if k == TAPS - 1:
+                            m = 4 * ip + 2 * il + mm
+                            res = rpool.tile([P, DIM], F32, name="res", tag="res")
+                            nc.scalar.activation(out=res[:], in_=acc[(il, mm)][:], func=ACTF.Copy, scale=norm[:, m : m + 1])
+                            nc.sync.dma_start(out=ov[m * P : (m + 1) * P, :], in_=res[:])
 
         def multiply(g):
             ip, tg = g // 3, g % 3
@@ -362,27 +338,35 @@ def tile_partialconvolution_kernel(tc, x, seg_mask, conv_w, out):
             keep_gate(rp0, 0, 36)
             prepare(0, sfill[0:FILL[0]])
             dot_classes(1, 2, esh[(1, 2)])
-            prepare(1, sfill[FILL[0]:FILL[1]])
             rp1 = replicate(36, 72, "acc")
             count_taps()
+            prepare(1, sfill[FILL[0]:FILL[1]])
+            keep_gate(rp1, 36, 72)
+            make_norm()
+        def weights(k):
+            if k in W_ON_VECTOR:
+                for part in range(VPARTS):
+                    regroup_w(k, part, VPARTS)
+            quantise_w(k)
+
         for g in range(6):
-            if g < 3:
-                for k in range(3 * g, 3 * g + 3):
-                    if k in W_ON_VECTOR:
-                        for part in range(VPARTS):
-                            regroup_w(k, part, VPARTS)
-                    quantise_w(k)
-            quantise_x(g)
-            if g == 0:
-                keep_gate(rp1, 36, 72)
-                make_norm()
-                if APATH:
-                    spread_gate()
-            multiply(g)
-            if APATH and g == RAWAT:
-                transpose_raw(0)
-                transpose_raw(1)
-            if APATH and g + 2 == 5:
-                prepare_late(5)
-            elif g + 2 < 6:
+            if TAPMAJOR and g < 5:
+                quantise_x(g, (0,))
+                if g < 3:
+                    weights(3 * g)
+                multiply_taps(g, (0,))
+                quantise_x(g, (1,))
+                if g < 3:
+                    weights(3 * g + 1)
+                multiply_taps(g, (1,))
+                if g < 3:
+                    weights(3 * g + 2)
+                multiply_taps(g, (2,))
+            else:
+                if g < 3:
+                    for k in range(3 * g, 3 * g + 3):
+                        weights(k)
+                quantise_x(g)
+                multiply(g)
+            if g + 2 < 6:
                 prepare(g + 2, sfill[FILL[g + 1]:FILL[g + 2]])

@@ -23,8 +23,8 @@ W_ON_VECTOR = (2, 5, 8)
 W_ON_GPSIMD = ()
 S_HEAD = (0, 1)
 S_FILL = (3, 4, 6, 7)
-LOADS = (0, -1, 1, 2, 3, 4, 5, 6, 7, 8, -2)
-FILL = (6, 12, 16, 16, 16, 16, 16)
+LOADS = (0, -1, 1, -2, 2, 3, 4, 5, 6, 7, 8, -3, -4)
+FILL = (0, 0, 0, 0, 0, 0, 0)
 VPARTS = 1
 WARM0 = 6
 WARM1 = 2
@@ -32,6 +32,11 @@ SUST = 2
 SUSTW = 512
 SPLIT_R = False
 TAPMAJOR = True
+DOT_EARLY = True
+BULK = (8, 16, 16, 16, 16, 16, 16)
+R1AT = 0
+CNTAT = 0
+KEEP_ON_S = False
 NDOT_EARLY = 1
 
 
@@ -52,17 +57,18 @@ def tile_partialconvolution_kernel(tc, x, seg_mask, conv_w, out):
         rpool = ctx.enter_context(tc.tile_pool(name="result", bufs=4))
         psum = ctx.enter_context(tc.psum_pool(name="psum", bufs=4))
 
-        m0 = const.tile([P, 8, NCLS], BF16, name="m0")
-        xs = [const.tile([P, 16, P], BF16, name="xs%d" % ip) for ip in range(2)]
+        m0 = [const.tile([P, 4, 32], BF16, name="m0%d" % ip) for ip in range(2)]
+        xs = [const.tile([P, 8, P], BF16, name="xs%d" % b) for b in range(4)]
         wraw = [const.tile([P, 4, DIM], BF16, name="wraw%d" % k) for k in range(TAPS)]
 
         def load_w(k):
             nc.sync.dma_start(out=wraw[k][:], in_=wv[:, :, k, :])
 
         def load_x(ip):
-            nc.sync.dma_start(out=xs[ip][:], in_=xv[:, 16 * ip : 16 * ip + 16, :])
+            nc.sync.dma_start(out=xs[ip][:], in_=xv[:, 8 * ip : 8 * ip + 8, :])
 
-        nc.sync.dma_start(out=m0[:], in_=sv)
+        for ip in range(2):
+            nc.sync.dma_start(out=m0[ip][:, :, 0:NCLS], in_=sv[:, 4 * ip : 4 * ip + 4, :])
         for item in LOADS:
             if item < 0:
                 load_x(-item - 1)
@@ -94,20 +100,25 @@ def tile_partialconvolution_kernel(tc, x, seg_mask, conv_w, out):
         rrep = const.tile([P, P, 4], F32, name="rrep")
         nc.vector.tensor_copy(out=rrep[:], in_=ident[:].unsqueeze(2).to_broadcast([P, P, 4]))
 
-        mx0 = const.tile([P, 8], F32, name="mx0")
-        e0 = const.tile([P, 8, NCLS], BF16, name="e0")
+        mx0 = [const.tile([P, 4], F32, name="mx0%d" % ip) for ip in range(2)]
+        e0 = [const.tile([P, 4, NCLS], BF16, name="e0%d" % ip) for ip in range(2)]
         prod = const.tile([P, 2, TAPS, 4, NCLS], BF16, name="prod")
         sels = const.tile([P, 2, TAPS, 4], F32, name="sels")
         nz = const.tile([P, 2, TAPS, 4], BF16, name="nz")
-        selr = const.tile([P, 4, 2 * TAPS * 4], F32, name="selr")
+        selr = const.tile([P, 4, TAPS * 4], F32, name="selr")
+        selr1 = const.tile([P, 4, TAPS * 4], F32, name="selr1")
         cmax = const.tile([P, 8], F32, name="cmax")
         crec = const.tile([P, 8], F32, name="crec")
         norm = const.tile([P, 8], F32, name="norm")
 
-        nc.vector.tensor_reduce(out=mx0[:], in_=m0[:], axis=AX.X, op=ALU.max)
-        nc.vector.tensor_tensor(
-            out=e0[:], in0=m0[:], in1=mx0[:].unsqueeze(2).to_broadcast([P, 8, NCLS]), op=ALU.is_equal
-        )
+        for ip in range(2):
+            nc.vector.tensor_reduce(out=mx0[ip][:], in_=m0[ip][:, :, 0:NCLS], axis=AX.X, op=ALU.max)
+            nc.vector.tensor_tensor(
+                out=e0[ip][:],
+                in0=m0[ip][:, :, 0:NCLS],
+                in1=mx0[ip][:].unsqueeze(2).to_broadcast([P, 4, NCLS]),
+                op=ALU.is_equal,
+            )
 
         cps = []
 
@@ -119,7 +130,7 @@ def tile_partialconvolution_kernel(tc, x, seg_mask, conv_w, out):
                 nc.tensor.matmul(
                     out=esh[:, kk, :, :],
                     lhsT=wide[:, kk, 128 - sh : 256 - sh],
-                    rhs=e0[:, 4 * ip : 4 * ip + 4, :],
+                    rhs=e0[ip][:],
                     start=True,
                     stop=(di == 0),
                 )
@@ -127,7 +138,7 @@ def tile_partialconvolution_kernel(tc, x, seg_mask, conv_w, out):
                     nc.tensor.matmul(
                         out=esh[:, kk, 1:4:2, :],
                         lhsT=wide[:, kk, 256 - sh : 384 - sh],
-                        rhs=e0[:, 4 * ip : 4 * ip + 4 : 2, :],
+                        rhs=e0[ip][:, 0:4:2, :],
                         start=False,
                         stop=True,
                     )
@@ -135,7 +146,7 @@ def tile_partialconvolution_kernel(tc, x, seg_mask, conv_w, out):
                     nc.tensor.matmul(
                         out=esh[:, kk, 0:4:2, :],
                         lhsT=wide[:, kk, -sh : 128 - sh],
-                        rhs=e0[:, 4 * ip + 1 : 4 * ip + 4 : 2, :],
+                        rhs=e0[ip][:, 1:4:2, :],
                         start=False,
                         stop=True,
                     )
@@ -146,7 +157,7 @@ def tile_partialconvolution_kernel(tc, x, seg_mask, conv_w, out):
             nc.vector.tensor_tensor(
                 out=prod[:, ip, ks, :, :],
                 in0=esh[:],
-                in1=m0[:, 4 * ip : 4 * ip + 4, :].unsqueeze(1).to_broadcast([P, 3, 4, NCLS]),
+                in1=m0[ip][:, :, 0:NCLS].unsqueeze(1).to_broadcast([P, 3, 4, NCLS]),
                 op=ALU.mult,
             )
             nc.vector.tensor_reduce(out=sels[:, ip, ks, :], in_=prod[:, ip, ks, :, :], axis=AX.X, op=ALU.add)
@@ -164,11 +175,16 @@ def tile_partialconvolution_kernel(tc, x, seg_mask, conv_w, out):
             return rp
 
         def keep_gate(rp, c0, c1):
-            nc.vector.tensor_copy(out=selr[:, :, c0:c1], in_=rp[:])
+            if c0 > 0 and KEEP_ON_S:
+                nc.scalar.copy(out=selr1[:], in_=rp[:])
+            elif c0 > 0:
+                nc.vector.tensor_copy(out=selr1[:], in_=rp[:])
+            else:
+                nc.vector.tensor_copy(out=selr[:], in_=rp[:])
 
         def count_taps():
             nc.vector.tensor_single_scalar(out=nz[:], in_=sels[:], scalar=0.0, op=ALU.not_equal)
-            cp = psum.tile([P, 2, 4], F32, name="cp", tag="acc")
+            cp = psum.tile([P, 2, 4], F32, name="cp", tag="tp")
             cps.append(cp)
             steps = []
             for k in range(TAPS):
@@ -226,9 +242,9 @@ def tile_partialconvolution_kernel(tc, x, seg_mask, conv_w, out):
                 gt = gpool.tile([P, 8, P], BF16, name="gt", tag="gt")
                 for nn in range(8):
                     n = 8 * b + nn
-                    col = 36 * ip + 4 * k + (n // 4) % 4
+                    col = 4 * k + (n // 4) % 4
                     nc.vector.tensor_scalar_mul(
-                        out=gt[:, nn, :], in0=xs[ip][:, n % 16, :], scalar1=selr[:, n % 4, col : col + 1]
+                        out=gt[:, nn, :], in0=xs[b][:, nn, :], scalar1=(selr, selr1)[ip][:, n % 4, col : col + 1]
                     )
                 pst = psum.tile([P, 1024], BF16, name="pst", tag="tp")
                 if g < 2 and u % SUST == 0:
@@ -333,24 +349,30 @@ def tile_partialconvolution_kernel(tc, x, seg_mask, conv_w, out):
             for tg in range(3):
                 dot_classes(0, tg, esh[(0, tg)])
             rp0 = replicate(0, 36, "tp")
-            dot_classes(1, 0, esh[(1, 0)])
-            dot_classes(1, 1, esh[(1, 1)])
+            for tg in range(3):
+                dot_classes(1, tg, esh[(1, tg)])
             keep_gate(rp0, 0, 36)
             prepare(0, sfill[0:FILL[0]])
-            dot_classes(1, 2, esh[(1, 2)])
-            rp1 = replicate(36, 72, "acc")
-            count_taps()
             prepare(1, sfill[FILL[0]:FILL[1]])
-            keep_gate(rp1, 36, 72)
-            make_norm()
+
         def weights(k):
             if k in W_ON_VECTOR:
                 for part in range(VPARTS):
                     regroup_w(k, part, VPARTS)
             quantise_w(k)
 
+        def bulk(a, b):
+            for f in sfill[a:b]:
+                regroup_w(f[0], f[1], 4)
+
+        bulk(FILL[1], BULK[0])
+        late = {}
         for g in range(6):
-            if TAPMAJOR and g < 5:
+            if g == R1AT:
+                late["rp1"] = replicate(36, 72, "tp")
+            if g == CNTAT:
+                count_taps()
+            if g < 5:
                 quantise_x(g, (0,))
                 if g < 3:
                     weights(3 * g)
@@ -363,10 +385,12 @@ def tile_partialconvolution_kernel(tc, x, seg_mask, conv_w, out):
                     weights(3 * g + 2)
                 multiply_taps(g, (2,))
             else:
-                if g < 3:
-                    for k in range(3 * g, 3 * g + 3):
-                        weights(k)
                 quantise_x(g)
                 multiply(g)
+            if g == R1AT:
+                keep_gate(late["rp1"], 36, 72)
+            if g == CNTAT:
+                make_norm()
             if g + 2 < 6:
-                prepare(g + 2, sfill[FILL[g + 1]:FILL[g + 2]])
+                prepare(g + 2, ())
+                bulk(BULK[g], BULK[g + 1])

@@ -23,8 +23,8 @@ W_ON_VECTOR = (2, 5, 8)
 W_ON_GPSIMD = ()
 S_HEAD = (0, 1)
 S_FILL = (3, 4, 6, 7)
-LOADS = (0, -1, 1, -2, 2, 3, 4, 5, 6, 7, 8, -3, -4)
-FILL = (0, 0, 0, 0, 0, 0, 0)
+LOADS = (0, -1, 1, 2, 3, 4, 5, 6, 7, 8, -2)
+FILL = (6, 12, 16, 16, 16, 16, 16)
 VPARTS = 1
 WARM0 = 6
 WARM1 = 2
@@ -32,11 +32,6 @@ SUST = 2
 SUSTW = 512
 SPLIT_R = False
 TAPMAJOR = True
-DOT_EARLY = True
-BULK = (8, 16, 16, 16, 16, 16, 16)
-R1AT = 0
-CNTAT = 0
-KEEP_ON_S = False
 NDOT_EARLY = 1
 
 
@@ -58,14 +53,14 @@ def tile_partialconvolution_kernel(tc, x, seg_mask, conv_w, out):
         psum = ctx.enter_context(tc.psum_pool(name="psum", bufs=4))
 
         m0 = [const.tile([P, 4, 32], BF16, name="m0%d" % ip) for ip in range(2)]
-        xs = [const.tile([P, 8, P], BF16, name="xs%d" % b) for b in range(4)]
+        xs = [const.tile([P, 16, P], BF16, name="xs%d" % ip) for ip in range(2)]
         wraw = [const.tile([P, 4, DIM], BF16, name="wraw%d" % k) for k in range(TAPS)]
 
         def load_w(k):
             nc.sync.dma_start(out=wraw[k][:], in_=wv[:, :, k, :])
 
         def load_x(ip):
-            nc.sync.dma_start(out=xs[ip][:], in_=xv[:, 8 * ip : 8 * ip + 8, :])
+            nc.sync.dma_start(out=xs[ip][:], in_=xv[:, 16 * ip : 16 * ip + 16, :])
 
         for ip in range(2):
             nc.sync.dma_start(out=m0[ip][:, :, 0:NCLS], in_=sv[:, 4 * ip : 4 * ip + 4, :])
@@ -105,8 +100,7 @@ def tile_partialconvolution_kernel(tc, x, seg_mask, conv_w, out):
         prod = const.tile([P, 2, TAPS, 4, NCLS], BF16, name="prod")
         sels = const.tile([P, 2, TAPS, 4], F32, name="sels")
         nz = const.tile([P, 2, TAPS, 4], BF16, name="nz")
-        selr = const.tile([P, 4, TAPS * 4], F32, name="selr")
-        selr1 = const.tile([P, 4, TAPS * 4], F32, name="selr1")
+        selr = const.tile([P, 4, 2 * TAPS * 4], F32, name="selr")
         cmax = const.tile([P, 8], F32, name="cmax")
         crec = const.tile([P, 8], F32, name="crec")
         norm = const.tile([P, 8], F32, name="norm")
@@ -175,16 +169,11 @@ def tile_partialconvolution_kernel(tc, x, seg_mask, conv_w, out):
             return rp
 
         def keep_gate(rp, c0, c1):
-            if c0 > 0 and KEEP_ON_S:
-                nc.scalar.copy(out=selr1[:], in_=rp[:])
-            elif c0 > 0:
-                nc.vector.tensor_copy(out=selr1[:], in_=rp[:])
-            else:
-                nc.vector.tensor_copy(out=selr[:], in_=rp[:])
+            nc.vector.tensor_copy(out=selr[:, :, c0:c1], in_=rp[:])
 
         def count_taps():
             nc.vector.tensor_single_scalar(out=nz[:], in_=sels[:], scalar=0.0, op=ALU.not_equal)
-            cp = psum.tile([P, 2, 4], F32, name="cp", tag="tp")
+            cp = psum.tile([P, 2, 4], F32, name="cp", tag="acc")
             cps.append(cp)
             steps = []
             for k in range(TAPS):
@@ -242,9 +231,9 @@ def tile_partialconvolution_kernel(tc, x, seg_mask, conv_w, out):
                 gt = gpool.tile([P, 8, P], BF16, name="gt", tag="gt")
                 for nn in range(8):
                     n = 8 * b + nn
-                    col = 4 * k + (n // 4) % 4
+                    col = 36 * ip + 4 * k + (n // 4) % 4
                     nc.vector.tensor_scalar_mul(
-                        out=gt[:, nn, :], in0=xs[b][:, nn, :], scalar1=(selr, selr1)[ip][:, n % 4, col : col + 1]
+                        out=gt[:, nn, :], in0=xs[ip][:, n % 16, :], scalar1=selr[:, n % 4, col : col + 1]
                     )
                 pst = psum.tile([P, 1024], BF16, name="pst", tag="tp")
                 if g < 2 and u % SUST == 0:
@@ -349,30 +338,24 @@ def tile_partialconvolution_kernel(tc, x, seg_mask, conv_w, out):
             for tg in range(3):
                 dot_classes(0, tg, esh[(0, tg)])
             rp0 = replicate(0, 36, "tp")
-            for tg in range(3):
-                dot_classes(1, tg, esh[(1, tg)])
+            dot_classes(1, 0, esh[(1, 0)])
+            dot_classes(1, 1, esh[(1, 1)])
             keep_gate(rp0, 0, 36)
             prepare(0, sfill[0:FILL[0]])
+            dot_classes(1, 2, esh[(1, 2)])
+            rp1 = replicate(36, 72, "acc")
+            count_taps()
             prepare(1, sfill[FILL[0]:FILL[1]])
-
+            keep_gate(rp1, 36, 72)
+            make_norm()
         def weights(k):
             if k in W_ON_VECTOR:
                 for part in range(VPARTS):
                     regroup_w(k, part, VPARTS)
             quantise_w(k)
 
-        def bulk(a, b):
-            for f in sfill[a:b]:
-                regroup_w(f[0], f[1], 4)
-
-        bulk(FILL[1], BULK[0])
-        late = {}
         for g in range(6):
-            if g == R1AT:
-                late["rp1"] = replicate(36, 72, "tp")
-            if g == CNTAT:
-                count_taps()
-            if g < 5:
+            if TAPMAJOR and g < 5:
                 quantise_x(g, (0,))
                 if g < 3:
                     weights(3 * g)
@@ -385,12 +368,10 @@ def tile_partialconvolution_kernel(tc, x, seg_mask, conv_w, out):
                     weights(3 * g + 2)
                 multiply_taps(g, (2,))
             else:
+                if g < 3:
+                    for k in range(3 * g, 3 * g + 3):
+                        weights(k)
                 quantise_x(g)
                 multiply(g)
-            if g == R1AT:
-                keep_gate(late["rp1"], 36, 72)
-            if g == CNTAT:
-                make_norm()
             if g + 2 < 6:
-                prepare(g + 2, ())
-                bulk(BULK[g], BULK[g + 1])
+                prepare(g + 2, sfill[FILL[g + 1]:FILL[g + 2]])

from contextlib import ExitStack

import concourse.mybir as mybir
from concourse.masks import make_identity

F32 = mybir.dt.float32
BF16 = mybir.dt.bfloat16
U32 = mybir.dt.uint32
U8 = mybir.dt.uint8
FP8X4 = mybir.dt.float8_e4m3fn_x4
ALU = mybir.AluOpType
ACTF = mybir.ActivationFunctionType
AX = mybir.AxisListType

P = 128
NCLS = 22
TAPS = 9
DIM = 512
FLOPS = 2 * 1024 * 4608 * 512

PINNED = True
W_ON_VECTOR = (2, 5, 8)
W_ON_GPSIMD = ()
S_HEAD = (0, 1)
S_FILL = (3, 4, 6, 7)
LOADS = (0, -1, 1, 2, 3, 4, 5, 6, 7, 8, -2)
FILL = (6, 12, 16, 16, 16, 16, 16)
VPARTS = 1
WARM0 = 6
WARM1 = 2
SUST = 2
SUSTW = 512
SPLIT_R = False
TAPMAJOR = True
NDOT_EARLY = 1


def tile_partialconvolution_kernel(tc, x, seg_mask, conv_w, out):
    nc = tc.nc
    xv = x.rearrange("b h w (t c) -> (b h w t) c", t=4).rearrange("(n q) c -> q n c", q=P)
    sv = seg_mask.rearrange("b h w c -> (b h w) c").rearrange("(m p) c -> p m c", p=P)
    wv = conv_w.rearrange("(t p) i j d -> p t (i j) d", p=P)
    ov = out.rearrange("b h w d -> (b h w) d")

    with ExitStack() as ctx:
        if PINNED:
            ctx.enter_context(tc.manual_schedule())
        const = ctx.enter_context(tc.tile_pool(name="const", bufs=1))
        gpool = ctx.enter_context(tc.tile_pool(name="gated", bufs=12))
        wgpool = ctx.enter_context(tc.tile_pool(name="wgrouped", bufs=9))
        xqpool = ctx.enter_context(tc.tile_pool(name="xquant", bufs=3))
        rpool = ctx.enter_context(tc.tile_pool(name="result", bufs=4))
        psum = ctx.enter_context(tc.psum_pool(name="psum", bufs=4))

        m0 = [const.tile([P, 4, 32], BF16, name="m0%d" % ip) for ip in range(2)]
        xs = [const.tile([P, 16, P], BF16, name="xs%d" % ip) for ip in range(2)]
        wraw = [const.tile([P, 4, DIM], BF16, name="wraw%d" % k) for k in range(TAPS)]

        def load_w(k):
            nc.sync.dma_start(out=wraw[k][:], in_=wv[:, :, k, :])

        def load_x(ip):
            nc.sync.dma_start(out=xs[ip][:], in_=xv[:, 16 * ip : 16 * ip + 16, :])

        for ip in range(2):
            nc.sync.dma_start(out=m0[ip][:, :, 0:NCLS], in_=sv[:, 4 * ip : 4 * ip + 4, :])
        for item in LOADS:
            if item < 0:
                load_x(-item - 1)
            else:
                load_w(item)

        zeros = const.tile([P, DIM], BF16, name="zeros")
        nc.vector.memset(zeros[:], 0.0)

        def warm(dst, times, width=DIM):
            for i in range(times):
                nc.tensor.matmul(out=dst, lhsT=zeros[:, 0:P], rhs=zeros[:, 0:width], start=True, stop=True)

        warmt = psum.tile([P, DIM], F32, name="warmt", tag="tp")
        warm(warmt[:], WARM0)
        ident = const.tile([P, P], BF16, name="ident")
        make_identity(nc, ident[:])
        wide = const.tile([P, 3, 384], BF16, name="wide")
        nc.vector.memset(wide[:], 0.0)
        gq = [const.tile([P, 6, 1024], BF16, name="gq%d" % tg, align_bytes=64) for tg in range(3)]
        nc.vector.memset(gq[0][:, :, 0:80], 0.0)
        nc.vector.memset(gq[1][:, :, 0:16], 0.0)
        nc.vector.memset(gq[1][:, :, 1008:1024], 0.0)
        nc.vector.memset(gq[2][:, :, 944:1024], 0.0)
        nc.vector.tensor_copy(out=wide[:, :, 128:256], in_=ident[:].unsqueeze(1).to_broadcast([P, 3, P]))
        w16 = wide[:, :, 128:256].rearrange("p j (a b) -> p j a b", b=16)
        nc.vector.memset(w16[:, 0, :, 0:1], 0.0)
        nc.vector.memset(w16[:, 2, :, 15:16], 0.0)
        rrep = const.tile([P, P, 4], F32, name="rrep")
        nc.vector.tensor_copy(out=rrep[:], in_=ident[:].unsqueeze(2).to_broadcast([P, P, 4]))

        mx0 = [const.tile([P, 4], F32, name="mx0%d" % ip) for ip in range(2)]
        e0 = [const.tile([P, 4, NCLS], BF16, name="e0%d" % ip) for ip in range(2)]
        prod = const.tile([P, 2, TAPS, 4, NCLS], BF16, name="prod")
        sels = const.tile([P, 2, TAPS, 4], F32, name="sels")
        nz = const.tile([P, 2, TAPS, 4], BF16, name="nz")
        selr = const.tile([P, 4, 2 * TAPS * 4], F32, name="selr")
        cmax = const.tile([P, 8], F32, name="cmax")
        crec = const.tile([P, 8], F32, name="crec")
        norm = const.tile([P, 8], F32, name="norm")

        for ip in range(2):
            nc.vector.tensor_reduce(out=mx0[ip][:], in_=m0[ip][:, :, 0:NCLS], axis=AX.X, op=ALU.max)
            nc.vector.tensor_tensor(
                out=e0[ip][:],
                in0=m0[ip][:, :, 0:NCLS],
                in1=mx0[ip][:].unsqueeze(2).to_broadcast([P, 4, NCLS]),
                op=ALU.is_equal,
            )

        cps = []

        def shift_onehot(ip, tg):
            esh = psum.tile([P, 3, 4, NCLS], F32, name="esh", tag=("tp" if ip == 0 else "acc"))
            di = tg - 1
            for kk in range(3):
                sh = 16 * di + kk - 1
                nc.tensor.matmul(
                    out=esh[:, kk, :, :],
                    lhsT=wide[:, kk, 128 - sh : 256 - sh],
                    rhs=e0[ip][:],
                    start=True,
                    stop=(di == 0),
                )
                if di == 1:
                    nc.tensor.matmul(
                        out=esh[:, kk, 1:4:2, :],
                        lhsT=wide[:, kk, 256 - sh : 384 - sh],
                        rhs=e0[ip][:, 0:4:2, :],
                        start=False,
                        stop=True,
                    )
                if di == -1:
                    nc.tensor.matmul(
                        out=esh[:, kk, 0:4:2, :],
                        lhsT=wide[:, kk, -sh : 128 - sh],
                        rhs=e0[ip][:, 1:4:2, :],
                        start=False,
                        stop=True,
                    )
            return esh

        def dot_classes(ip, tg, esh):
            ks = slice(3 * tg, 3 * tg + 3)
            nc.vector.tensor_tensor(
                out=prod[:, ip, ks, :, :],
                in0=esh[:],
                in1=m0[ip][:, :, 0:NCLS].unsqueeze(1).to_broadcast([P, 3, 4, NCLS]),
                op=ALU.mult,
            )
            nc.vector.tensor_reduce(out=sels[:, ip, ks, :], in_=prod[:, ip, ks, :, :], axis=AX.X, op=ALU.add)

        def replicate(c0, c1, tag):
            rp = psum.tile([P, 4, c1 - c0], F32, name="rp", tag=tag)
            for g in range(4):
                nc.tensor.matmul(
                    out=rp[:, g, :],
                    lhsT=rrep[:, 32 * g : 32 * g + 32, :].rearrange("p a t -> p (a t)"),
                    rhs=sels[:].rearrange("p i k m -> p (i k m)")[:, c0:c1],
                    start=True,
                    stop=True,
                )
            return rp

        def keep_gate(rp, c0, c1):
            nc.vector.tensor_copy(out=selr[:, :, c0:c1], in_=rp[:])

        def count_taps():
            nc.vector.tensor_single_scalar(out=nz[:], in_=sels[:], scalar=0.0, op=ALU.not_equal)
            cp = psum.tile([P, 2, 4], F32, name="cp", tag="acc")
            cps.append(cp)
            steps = []
            for k in range(TAPS):
                di = k // 3 - 1
                sh = 16 * di + k % 3 - 1
                steps.append((cp[:, :, :], 128 + sh, nz[:, :, k, :]))
                if di == 1:
                    steps.append((cp[:, :, 0:4:2], sh, nz[:, :, k, 1:4:2]))
                if di == -1:
                    steps.append((cp[:, :, 1:4:2], 256 + sh, nz[:, :, k, 0:4:2]))
            for i, (o, c0, r) in enumerate(steps):
                nc.tensor.matmul(
                    out=o, lhsT=wide[:, 1, c0 : c0 + P], rhs=r, start=(i == 0), stop=(i == len(steps) - 1)
                )

        def make_norm():
            cp = cps[0]
            nc.vector.tensor_scalar_max(out=cmax[:], in0=cp[:].rearrange("p a b -> p (a b)"), scalar1=1.0)
            nc.vector.reciprocal(out=crec[:], in_=cmax[:])
            nc.vector.tensor_scalar_mul(out=norm[:], in0=crec[:], scalar1=9.0)

        wq = const.tile([P, TAPS, DIM], U32, name="wq", align_bytes=64)
        ws = const.tile([P, TAPS, DIM], U8, name="ws", align_bytes=64)
        wg = {}

        def regroup_w(k, part, parts):
            if part == 0:
                wg[k] = wgpool.tile([P, DIM, 4], BF16, name="wg", tag="wg", align_bytes=64)
            n = DIM // parts
            dst = wg[k][:, part * n : (part + 1) * n, :].rearrange("p (c i) t -> p c t i", i=4)
            src = wraw[k][:, :, part * n : (part + 1) * n].rearrange("p t (c i) -> p c t i", i=4)
            if k in W_ON_VECTOR:
                nc.vector.tensor_copy(out=dst, in_=src)
            elif k in W_ON_GPSIMD:
                nc.gpsimd.tensor_scalar(out=dst, in0=src, scalar1=1.0, scalar2=0.0, op0=ALU.mult, op1=ALU.add)
            else:
                nc.scalar.copy(out=dst, in_=src)

        def quantise_w(k):
            nc.vector.quantize_mx(
                out=wq[:, k, :].bitcast(FP8X4), scales=ws[:, k, :], in_=wg[k][:].rearrange("p d t -> p (d t)")
            )

        xq = {}
        xsc = {}
        acc = {}

        def prepare(g, fill=()):
            fill = list(fill)
            ip, tg = g // 3, g % 3
            for u in range(6):
                il, kk = u // 3, u % 3
                b, k = 2 * ip + il, 3 * tg + kk
                sh = 16 * (tg - 1) + kk - 1
                gt = gpool.tile([P, 8, P], BF16, name="gt", tag="gt")
                for nn in range(8):
                    n = 8 * b + nn
                    col = 36 * ip + 4 * k + (n // 4) % 4
                    nc.vector.tensor_scalar_mul(
                        out=gt[:, nn, :], in0=xs[ip][:, n % 16, :], scalar1=selr[:, n % 4, col : col + 1]
                    )
                pst = psum.tile([P, 1024], BF16, name="pst", tag="tp")
                if g < 2 and u % SUST == 0:
                    warm(pst[:, 0:SUSTW], 1, SUSTW)
                for nn in range(8):
                    nc.tensor.transpose(out=pst[:, nn * P : (nn + 1) * P], in_=gt[:, nn, :], identity=ident[:])
                d0, d1 = max(0, -sh), min(256, 256 - sh)
                nc.scalar.copy(out=gq[tg][:, u, 4 * d0 : 4 * d1], in_=pst[:, 4 * (d0 + sh) : 4 * (d1 + sh)])
                for f in fill[u * len(fill) // 6 : (u + 1) * len(fill) // 6]:
                    regroup_w(f[0], f[1], 4)

        def quantise_x(g, halves=(0, 1)):
            tg = g % 3
            if 0 in halves:
                xq[g] = xqpool.tile([P, 6, 256], U32, name="xq", tag="xq", align_bytes=64)
                xsc[g] = xqpool.tile([P, 6, 256], U8, name="xsc", tag="xsc", align_bytes=64)
            for u0, u1 in [((0, 4), (4, 6))[h] for h in halves]:
                nc.vector.quantize_mx(
                    out=xq[g][:, u0:u1, :].rearrange("p u w -> p (u w)").bitcast(FP8X4),
                    scales=xsc[g][:, u0:u1, :].rearrange("p u w -> p (u w)"),
                    in_=gq[tg][:, u0:u1, :].rearrange("p u w -> p (u w)"),
                )

        def multiply_taps(g, kks):
            ip, tg = g // 3, g % 3
            for kk in kks:
                for il in range(2):
                    for mm in range(2):
                        if tg == 0 and kk == 0:
                            acc[(il, mm)] = psum.tile([P, DIM], F32, name="acc", tag="acc")
                        u, k = 3 * il + kk, 3 * tg + kk
                        nc.tensor.matmul_mx(
                            out=acc[(il, mm)][:],
                            lhsT=xq[g][:, u, mm * P : (mm + 1) * P].bitcast(FP8X4),
                            lhsT_scale=xsc[g][:, u, mm * P : (mm + 1) * P],
                            rhs=wq[:, k, :].bitcast(FP8X4),
                            rhs_scale=ws[:, k, :],
                            start=(k == 0),
                            stop=(k == TAPS - 1),
                        )
                        if k == TAPS - 1:
                            m = 4 * ip + 2 * il + mm
                            res = rpool.tile([P, DIM], F32, name="res", tag="res")
                            nc.scalar.activation(out=res[:], in_=acc[(il, mm)][:], func=ACTF.Copy, scale=norm[:, m : m + 1])
                            nc.sync.dma_start(out=ov[m * P : (m + 1) * P, :], in_=res[:])

        def multiply(g):
            ip, tg = g // 3, g % 3
            for il in range(2):
                for mm in range(2):
                    if tg == 0:
                        acc[(il, mm)] = psum.tile([P, DIM], F32, name="acc", tag="acc")
                    for kk in range(3):
                        u, k = 3 * il + kk, 3 * tg + kk
                        nc.tensor.matmul_mx(
                            out=acc[(il, mm)][:],
                            lhsT=xq[g][:, u, mm * P : (mm + 1) * P].bitcast(FP8X4),
                            lhsT_scale=xsc[g][:, u, mm * P : (mm + 1) * P],
                            rhs=wq[:, k, :].bitcast(FP8X4),
                            rhs_scale=ws[:, k, :],
                            start=(k == 0),
                            stop=(k == TAPS - 1),
                        )
                    if tg == 2:
                        m = 4 * ip + 2 * il + mm
                        res = rpool.tile([P, DIM], F32, name="res", tag="res")
                        nc.scalar.activation(out=res[:], in_=acc[(il, mm)][:], func=ACTF.Copy, scale=norm[:, m : m + 1])
                        nc.sync.dma_start(out=ov[m * P : (m + 1) * P, :], in_=res[:])

        esh = {}
        for ip in range(2):
            for tg in range(3):
                esh[(ip, tg)] = shift_onehot(ip, tg)
        warm(warmt[:], WARM1)
        for k in W_ON_GPSIMD:
            regroup_w(k, 0, 1)
        for k in S_HEAD:
            for part in range(4):
                regroup_w(k, part, 4)
        sfill = [(k, part) for k in S_FILL for part in range(4)]
        if SPLIT_R:
            dot_classes(0, 0, esh[(0, 0)])
            rpa = replicate(0, 12, "tp")
            dot_classes(0, 1, esh[(0, 1)])
            dot_classes(0, 2, esh[(0, 2)])
            for tg in range(NDOT_EARLY):
                dot_classes(1, tg, esh[(1, tg)])
            keep_gate(rpa, 0, 12)
            if NDOT_EARLY == 3:
                rpb = replicate(12, 72, "acc")
                count_taps()
            prepare(0, sfill[0:FILL[0]])
            for tg in range(NDOT_EARLY, 3):
                dot_classes(1, tg, esh[(1, tg)])
            if NDOT_EARLY < 3:
                rpb = replicate(12, 72, "acc")
                count_taps()
            keep_gate(rpb, 12, 72)
            prepare(1, sfill[FILL[0]:FILL[1]])
            make_norm()
        else:
            for tg in range(3):
                dot_classes(0, tg, esh[(0, tg)])
            rp0 = replicate(0, 36, "tp")
            dot_classes(1, 0, esh[(1, 0)])
            dot_classes(1, 1, esh[(1, 1)])
            keep_gate(rp0, 0, 36)
            prepare(0, sfill[0:FILL[0]])
            dot_classes(1, 2, esh[(1, 2)])
            rp1 = replicate(36, 72, "acc")
            count_taps()
            prepare(1, sfill[FILL[0]:FILL[1]])
            keep_gate(rp1, 36, 72)
            make_norm()
        def weights(k):
            if k in W_ON_VECTOR:
                for part in range(VPARTS):
                    regroup_w(k, part, VPARTS)
            quantise_w(k)

        for g in range(6):
            if TAPMAJOR and g < 5:
                quantise_x(g, (0,))
                if g < 3:
                    weights(3 * g)
                multiply_taps(g, (0,))
                quantise_x(g, (1,))
                if g < 3:
                    weights(3 * g + 1)
                multiply_taps(g, (1,))
                if g < 3:
                    weights(3 * g + 2)
                multiply_taps(g, (2,))
            else:
                if g < 3:
                    for k in range(3 * g, 3 * g + 3):
                        weights(k)
                quantise_x(g)
                multiply(g)
            if g + 2 < 6:
                prepare(g + 2, sfill[FILL[g + 1]:FILL[g + 2]])
